import numpy as np
import ml_dtypes


def mxq(x, axis, fmt="e4m3"):
    dtype, down = {"e4m3": (ml_dtypes.float8_e4m3fn, 7), "e5m2": (ml_dtypes.float8_e5m2, 14)}[fmt]
    v = np.moveaxis(np.asarray(x, np.float32).astype(ml_dtypes.bfloat16).astype(np.float64), axis, -1)
    blocks = v.reshape(v.shape[:-1] + (-1, 32))
    amax = np.abs(blocks).max(-1, keepdims=True)
    byte = np.maximum(np.where(amax > 0, np.frexp(amax)[1] - 1 + 127, 0) - down, 1)
    scale = np.exp2(byte - 127.0)
    codes = (blocks / scale).astype(np.float32).astype(dtype).astype(np.float64)
    return np.moveaxis((codes * scale).reshape(v.shape), -1, axis)


WIDE = False


def mx_kscale(k):
    if not WIDE:
        return np.ones(k)
    levels = np.array([20, -20, 10, -10, 0])
    a = np.random.permutation(np.resize(levels, k // 512 * 4)).reshape(k // 512, 4)
    idx = np.arange(k)
    return np.exp2(a[idx // 512, idx % 128 // 32])


BF16 = ml_dtypes.bfloat16


def bf(x):
    return np.asarray(x, np.float32).astype(BF16)


def f64(x):
    return np.asarray(x).astype(np.float64)


B, S, I, O = 1, 512, 2048, 4096

PRIMAL_LUT = np.array([0.0, 1.0, -1.0, 0.5, -0.5, 0.333333, -0.333333, 0.2, -0.2,
                       0.142857, -0.142857, 0.090909, -0.090909, 0.076923, -0.076923, 0.0],
                      dtype=np.float32).astype(np.float64)


def primal_quantize(weight, scale):
    w_scaled = weight / scale
    best_dist = np.full_like(w_scaled, np.inf)
    q = np.zeros_like(w_scaled)
    for v in PRIMAL_LUT:
        d = np.abs(w_scaled - v)
        take = d < best_dist
        best_dist = np.where(take, d, best_dist)
        q = np.where(take, v, q)
    return q * scale


def setup_inputs():
    s = mx_kscale(O)
    used = s == s.min()
    sc = float(np.exp2(-np.random.randint(4, 7))) / float(s.min())
    x = np.random.standard_normal((B, S, I))
    weight = np.random.standard_normal((O, I)) * 0.4 * sc * np.where(used, 1.0, 2.0 ** -8)[:, None]
    g = np.random.standard_normal((B, S, O)) * np.exp2(np.random.randint(-12, 1, (B, S, 1))) * 16.0 * s
    return {"x": bf(x), "weight": bf(weight), "scale": bf(np.array([sc])), "grad_out": bf(g)}


def reference(x, weight, scale, grad_out):
    w_quant = primal_quantize(f64(weight), f64(scale))
    return mxq(f64(grad_out), 2, "e5m2") @ mxq(w_quant, 0, "e4m3")

@@ -1,0 +1,158 @@
+from contextlib import ExitStack
+
+import concourse.bass as bass
+import concourse.mybir as mybir
+import concourse.tile as tile
+from concourse.masks import make_identity
+
+F32 = mybir.dt.float32
+BF16 = mybir.dt.bfloat16
+U32 = mybir.dt.uint32
+U8 = mybir.dt.uint8
+E4X4 = mybir.dt.float8_e4m3fn_x4
+E5X4 = mybir.dt.float8_e5m2_x4
+ALU = mybir.AluOpType
+ACT = mybir.ActivationFunctionType
+
+P = 128
+S, O, I = 512, 4096, 2048
+K_PASS = 512
+PASSES = O // K_PASS
+S_TILES = S // P
+W = 1024
+HALVES = I // W
+N_TILE = 512
+I_TILES = W // N_TILE
+
+FLOPS = 2 * S * O * I
+BYTES = O * I * 2 + S * O * 2 + 2 + S * I * 4
+
+VALUES = [0.076923, 0.090909, 0.142857, 0.2, 0.333333, 0.5, 1.0]
+EDGES = [0.03846149891614914, 0.08391599729657173, 0.11688299849629402, 0.17142850160598755,
+         0.2666664943099022, 0.41666649281978607, 0.75]
+L = 7
+
+
+def tile_primallinear_kernel(tc, x, weight, scale, grad_out, out):
+    nc = tc.nc
+    g2d = grad_out.rearrange("b s o -> (b s) o")
+    o2d = out.rearrange("b s i -> (b s) i")
+    with ExitStack() as ctx:
+        keep = ctx.enter_context(tc.tile_pool(name="keep", bufs=1))
+        wr_pool = ctx.enter_context(tc.tile_pool(name="wr", bufs=3))
+        ag_pool = ctx.enter_context(tc.tile_pool(name="ag", bufs=2))
+        sg_pool = ctx.enter_context(tc.tile_pool(name="sg", bufs=3))
+        tmp = ctx.enter_context(tc.tile_pool(name="tmp", bufs=1))
+        two = ctx.enter_context(tc.tile_pool(name="two", bufs=2))
+        gr_pool = ctx.enter_context(tc.tile_pool(name="gr", bufs=3))
+        ost = ctx.enter_context(tc.tile_pool(name="ost", bufs=4))
+        psum = ctx.enter_context(tc.psum_pool(name="ps", bufs=8))
+
+        sc_bf = keep.tile([P, 1], BF16)
+        nc.sync.dma_start(out=sc_bf[:], in_=scale.partition_broadcast(P))
+        sc = keep.tile([P, 1], F32)
+        nc.vector.tensor_copy(out=sc[:], in_=sc_bf[:])
+        cst = keep.tile([P, 16], F32)
+        for j in range(L):
+            nc.vector.tensor_scalar(out=cst[:, j:j + 1], in0=sc[:, 0:1], scalar1=EDGES[j], scalar2=None, op0=ALU.mult)
+            nc.vector.tensor_scalar(out=cst[:, 8 + j:9 + j], in0=sc[:, 0:1], scalar1=VALUES[j], scalar2=None, op0=ALU.mult)
+        ident = keep.tile([P, P], F32)
+        make_identity(nc, ident[:])
+
+        g_codes = keep.tile([P, PASSES, S], U32, align_bytes=64)
+        g_scales = keep.tile([P, PASSES, S], U8, align_bytes=64)
+
+        def load_w(h, c):
+            wr = wr_pool.tile([P, 4, W], BF16, name="wr")
+            for u in range(2):
+                r0 = K_PASS * c + 256 * u
+                nc.sync.dma_start(
+                    out=wr[:, 2 * u:2 * u + 2, :],
+                    in_=weight[r0:r0 + 256, h * W:(h + 1) * W].rearrange("(p e) w -> p e w", e=2),
+                )
+            return wr
+
+        def split_w(wr):
+            ag = ag_pool.tile([P, W, 4], BF16, name="ag")
+            sg = sg_pool.tile([P, W, 4], BF16, name="sg")
+            src = wr[:].rearrange("p t (c i) -> p c t i", i=4)
+            nc.scalar.activation(out=ag[:].rearrange("p (c i) t -> p c t i", i=4), in_=src, func=ACT.Abs)
+            nc.scalar.activation(out=sg[:].rearrange("p (c i) t -> p c t i", i=4), in_=src, func=ACT.Sign)
+            return ag, sg
+
+        def plane(dst, a, j):
+            nc.vector.tensor_scalar(out=dst, in0=a, scalar1=cst[:, j:j + 1], scalar2=cst[:, 8 + j:9 + j],
+                                    op0=ALU.is_ge, op1=ALU.mult)
+
+        def vmax(dst, a, b):
+            nc.vector.tensor_tensor(out=dst, in0=a, in1=b, op=ALU.max)
+
+        def g_pass(c):
+            gr = gr_pool.tile([P, S_TILES, K_PASS], BF16, name="gr")
+            nc.sync.dma_start(out=gr[:], in_=g2d[:, K_PASS * c:K_PASS * (c + 1)].rearrange("(s p) k -> p s k", p=P))
+            gg = two.tile([P, 4 * S], BF16, name="gg", align_bytes=64)
+            ggw = gg[:].bitcast(F32)
+            for sp in range(2):
+                tp = psum.tile([P, 512], F32, name="bank")
+                for s2 in range(2):
+                    words = gr[:, 2 * sp + s2, :].bitcast(F32)
+                    for u in range(2):
+                        o0 = (2 * s2 + u) * P
+                        nc.tensor.transpose(tp[:, o0:o0 + P], words[:, P * u:P * (u + 1)], ident[:])
+                nc.scalar.copy(
+                    out=ggw[:, sp * 512:(sp + 1) * 512].rearrange("p (s r u) -> p s r u", s=2, u=2),
+                    in_=tp[:].rearrange("p (s u r) -> p s r u", s=2, u=2),
+                )
+            nc.vector.quantize_mx(out=g_codes[:, c, :].bitcast(E5X4), scales=g_scales[:, c, :], in_=gg[:])
+
+        chunks = [(h, c) for h in range(HALVES) for c in range(PASSES)]
+        wr0 = load_w(*chunks[0])
+        pre = {0: split_w(wr0)}
+        for c in range(PASSES):
+            g_pass(c)
+
+        acc = {}
+        for n, (h, c) in enumerate(chunks):
+            if n + 1 < len(chunks):
+                pre[n + 1] = split_w(load_w(*chunks[n + 1]))
+            ag, sg = pre.pop(n)
+            a = ag[:].rearrange("p w t -> p (w t)")
+            f = [tmp.tile([P, 4 * W], BF16, name="f%d" % k) for k in range(5)]
+            plane(f[0][:], a, 0)
+            plane(f[1][:], a, 1)
+            plane(f[2][:], a, 2)
+            plane(f[3][:], a, 3)
+            vmax(f[0][:], f[0][:], f[1][:])
+            vmax(f[2][:], f[2][:], f[3][:])
+            plane(f[1][:], a, 4)
+            plane(f[3][:], a, 5)
+            plane(f[4][:], a, 6)
+            vmax(f[0][:], f[0][:], f[2][:])
+            vmax(f[1][:], f[1][:], f[3][:])
+            vmax(f[0][:], f[0][:], f[4][:])
+            vmax(f[0][:], f[0][:], f[1][:])
+            wq = two.tile([P, 4 * W], BF16, name="wq", align_bytes=64)
+            nc.vector.tensor_tensor(out=wq[:], in0=f[0][:], in1=sg[:].rearrange("p w t -> p (w t)"), op=ALU.mult)
+            w_codes = two.tile([P, W], U32, name="w_codes", align_bytes=64)
+            w_scales = two.tile([P, W], U8, name="w_scales", align_bytes=64)
+            nc.vector.quantize_mx(out=w_codes[:].bitcast(E4X4), scales=w_scales[:], in_=wq[:])
+            for it in range(I_TILES):
+                for s in range(S_TILES):
+                    if c == 0:
+                        acc[(s, it)] = psum.tile([P, 512], F32, name="bank")
+                    nc.tensor.matmul_mx(
+                        out=acc[(s, it)][:],
+                        lhsT=g_codes[:, c, s * P:(s + 1) * P].bitcast(E5X4),
+                        lhsT_scale=g_scales[:, c, s * P:(s + 1) * P],
+                        rhs=w_codes[:, it * N_TILE:(it + 1) * N_TILE].bitcast(E4X4),
+                        rhs_scale=w_scales[:, it * N_TILE:(it + 1) * N_TILE],
+                        start=(c == 0),
+                        stop=(c == PASSES - 1),
+                    )
+            if c == PASSES - 1:
+                for it in range(I_TILES):
+                    for s in range(S_TILES):
+                        res = ost.tile([P, N_TILE], F32, name="res")
+                        nc.scalar.copy(out=res[:], in_=acc[(s, it)][:])
+                        c0 = h * W + it * N_TILE
+                        nc.sync.dma_start(out=o2d[s * P:(s + 1) * P, c0:c0 + N_TILE], in_=res[:])

@@ -1,8 +1,6 @@
 from contextlib import ExitStack
 
-import concourse.bass as bass
 import concourse.mybir as mybir
-import concourse.tile as tile
 from concourse.masks import make_identity
 
 F32 = mybir.dt.float32
@@ -28,9 +26,9 @@ FLOPS = 2 * S * O * I
 BYTES = O * I * 2 + S * O * 2 + 2 + S * I * 4
 
 VALUES = [0.076923, 0.090909, 0.142857, 0.2, 0.333333, 0.5, 1.0]
-EDGES = [0.03846149891614914, 0.08391599729657173, 0.11688299849629402, 0.17142850160598755,
-         0.2666664943099022, 0.41666649281978607, 0.75]
-L = 7
+EDGES = [0.0384521484375, 0.083740234375, 0.116943359375, 0.17138671875, 0.2666015625, 0.4169921875, 0.748046875]
+PAIRS = [(0, 1), (2, 3), (4, 5)]
+MAGIC = 12582912.0
 
 
 def tile_primallinear_kernel(tc, x, weight, scale, grad_out, out):
@@ -40,11 +38,9 @@ def tile_primallinear_kernel(tc, x, weight, scale, grad_out, out):
     with ExitStack() as ctx:
         keep = ctx.enter_context(tc.tile_pool(name="keep", bufs=1))
         wr_pool = ctx.enter_context(tc.tile_pool(name="wr", bufs=3))
-        ag_pool = ctx.enter_context(tc.tile_pool(name="ag", bufs=2))
-        sg_pool = ctx.enter_context(tc.tile_pool(name="sg", bufs=3))
+        act_pool = ctx.enter_context(tc.tile_pool(name="actp", bufs=2))
         tmp = ctx.enter_context(tc.tile_pool(name="tmp", bufs=1))
         two = ctx.enter_context(tc.tile_pool(name="two", bufs=2))
-        gr_pool = ctx.enter_context(tc.tile_pool(name="gr", bufs=3))
         ost = ctx.enter_context(tc.tile_pool(name="ost", bufs=4))
         psum = ctx.enter_context(tc.psum_pool(name="ps", bufs=8))
 
@@ -52,91 +48,133 @@ def tile_primallinear_kernel(tc, x, weight, scale, grad_out, out):
         nc.sync.dma_start(out=sc_bf[:], in_=scale.partition_broadcast(P))
         sc = keep.tile([P, 1], F32)
         nc.vector.tensor_copy(out=sc[:], in_=sc_bf[:])
+        inv = keep.tile([P, 1], F32)
+        nc.vector.reciprocal(out=inv[:], in_=sc[:])
         cst = keep.tile([P, 16], F32)
-        for j in range(L):
-            nc.vector.tensor_scalar(out=cst[:, j:j + 1], in0=sc[:, 0:1], scalar1=EDGES[j], scalar2=None, op0=ALU.mult)
-            nc.vector.tensor_scalar(out=cst[:, 8 + j:9 + j], in0=sc[:, 0:1], scalar1=VALUES[j], scalar2=None, op0=ALU.mult)
+
+        def col(j):
+            return cst[:, j:j + 1]
+
+        for k, (lo, hi) in enumerate(PAIRS):
+            h = EDGES[hi] - EDGES[lo]
+            nc.vector.tensor_scalar(out=col(k), in0=inv[:, 0:1], scalar1=1.0 / h, scalar2=None, op0=ALU.mult)
+            nc.vector.tensor_scalar(out=col(3 + k), in0=sc[:, 0:1], scalar1=0.0, scalar2=0.5 - EDGES[lo] / h,
+                                    op0=ALU.mult, op1=ALU.add)
+            nc.vector.tensor_scalar(out=col(6 + k), in0=sc[:, 0:1], scalar1=VALUES[lo], scalar2=None, op0=ALU.mult)
+            nc.vector.tensor_scalar(out=col(9 + k), in0=sc[:, 0:1], scalar1=VALUES[hi], scalar2=None, op0=ALU.mult)
+        nc.vector.tensor_scalar(out=col(12), in0=sc[:, 0:1], scalar1=EDGES[6], scalar2=None, op0=ALU.mult)
+        nc.vector.tensor_scalar(out=col(13), in0=sc[:, 0:1], scalar1=VALUES[6], scalar2=None, op0=ALU.mult)
         ident = keep.tile([P, P], F32)
         make_identity(nc, ident[:])
 
         g_codes = keep.tile([P, PASSES, S], U32, align_bytes=64)
         g_scales = keep.tile([P, PASSES, S], U8, align_bytes=64)
 
-        def load_w(h, c):
+        def load_w(h, c, c0, wd):
             wr = wr_pool.tile([P, 4, W], BF16, name="wr")
             for u in range(2):
                 r0 = K_PASS * c + 256 * u
                 nc.sync.dma_start(
-                    out=wr[:, 2 * u:2 * u + 2, :],
-                    in_=weight[r0:r0 + 256, h * W:(h + 1) * W].rearrange("(p e) w -> p e w", e=2),
+                    out=wr[:, 2 * u:2 * u + 2, :wd],
+                    in_=weight[r0:r0 + 256, h * W + c0:h * W + c0 + wd].rearrange("(p e) w -> p e w", e=2),
                 )
             return wr
 
-        def split_w(wr):
-            ag = ag_pool.tile([P, W, 4], BF16, name="ag")
-            sg = sg_pool.tile([P, W, 4], BF16, name="sg")
-            src = wr[:].rearrange("p t (c i) -> p c t i", i=4)
-            nc.scalar.activation(out=ag[:].rearrange("p (c i) t -> p c t i", i=4), in_=src, func=ACT.Abs)
-            nc.scalar.activation(out=sg[:].rearrange("p (c i) t -> p c t i", i=4), in_=src, func=ACT.Sign)
-            return ag, sg
+        def scalar_part(wr, wd):
+            n = 4 * wd
+            ag = act_pool.tile([P, 4 * W], BF16, name="ag")
+            sg = act_pool.tile([P, 4 * W], BF16, name="sg")
+            y0 = act_pool.tile([P, 4 * W], BF16, name="y0")
+            y1 = act_pool.tile([P, 4 * W], BF16, name="y1")
+            src = wr[:, :, :wd].rearrange("p t (c i) -> p c t i", i=4)
+            nc.scalar.activation(out=ag[:, :n].rearrange("p (c i t) -> p c t i", i=4, t=4), in_=src, func=ACT.Abs)
+            nc.scalar.activation(out=y0[:, :n], in_=ag[:, :n], func=ACT.Identity, scale=col(0), bias=col(3))
+            nc.scalar.activation(out=y1[:, :n], in_=ag[:, :n], func=ACT.Identity, scale=col(1), bias=col(4))
+            nc.scalar.activation(out=sg[:, :n].rearrange("p (c i t) -> p c t i", i=4, t=4), in_=src, func=ACT.Sign)
+            return ag, sg, y0, y1
 
-        def plane(dst, a, j):
-            nc.vector.tensor_scalar(out=dst, in0=a, scalar1=cst[:, j:j + 1], scalar2=cst[:, 8 + j:9 + j],
-                                    op0=ALU.is_ge, op1=ALU.mult)
+        def g_pass(c):
+            gr = wr_pool.tile([P, 4, W], BF16, name="wr")
+            nc.sync.dma_start(out=gr[:, :, :K_PASS],
+                              in_=g2d[:, K_PASS * c:K_PASS * (c + 1)].rearrange("(s p) k -> p s k", p=P))
+            gg = two.tile([P, 4 * W], BF16, name="wq", align_bytes=64)
+            ggw = gg[:, :4 * S].bitcast(F32)
+            for sp in range(2):
+                tp = psum.tile([P, 512], F32, name="bank")
+                for s2 in range(2):
+                    words = gr[:, 2 * sp + s2, :K_PASS].bitcast(F32)
+                    for u in range(2):
+                        o0 = (2 * s2 + u) * P
+                        nc.tensor.transpose(tp[:, o0:o0 + P], words[:, P * u:P * (u + 1)], ident[:])
+                nc.vector.tensor_copy(
+                    out=ggw[:, sp * 512:(sp + 1) * 512].rearrange("p (s r u) -> p s r u", s=2, u=2),
+                    in_=tp[:].rearrange("p (s u r) -> p s r u", s=2, u=2),
+                )
+            nc.vector.quantize_mx(out=g_codes[:, c, :].bitcast(E5X4), scales=g_scales[:, c, :], in_=gg[:, :4 * S])
+
+        def ts(dst, src, s1, s2, op0, op1):
+            nc.vector.tensor_scalar(out=dst, in0=src, scalar1=s1, scalar2=s2, op0=op0, op1=op1)
 
         def vmax(dst, a, b):
             nc.vector.tensor_tensor(out=dst, in0=a, in1=b, op=ALU.max)
 
-        def g_pass(c):
-            gr = gr_pool.tile([P, S_TILES, K_PASS], BF16, name="gr")
-            nc.sync.dma_start(out=gr[:], in_=g2d[:, K_PASS * c:K_PASS * (c + 1)].rearrange("(s p) k -> p s k", p=P))
-            gg = two.tile([P, 4 * S], BF16, name="gg", align_bytes=64)
-            ggw = gg[:].bitcast(F32)
-            for sp in range(2):
-                tp = psum.tile([P, 512], F32, name="bank")
-                for s2 in range(2):
-                    words = gr[:, 2 * sp + s2, :].bitcast(F32)
-                    for u in range(2):
-                        o0 = (2 * s2 + u) * P
-                        nc.tensor.transpose(tp[:, o0:o0 + P], words[:, P * u:P * (u + 1)], ident[:])
-                nc.scalar.copy(
-                    out=ggw[:, sp * 512:(sp + 1) * 512].rearrange("p (s r u) -> p s r u", s=2, u=2),
-                    in_=tp[:].rearrange("p (s u r) -> p s r u", s=2, u=2),
-                )
-            nc.vector.quantize_mx(out=g_codes[:, c, :].bitcast(E5X4), scales=g_scales[:, c, :], in_=gg[:])
+        units = []
+        for h in range(HALVES):
+            for c in range(PASSES):
+                if (h, c) == (0, 0):
+                    cuts = [256, 256, 512]
+                elif (h, c) == (HALVES - 1, PASSES - 1):
+                    cuts = [512, 512]
+                else:
+                    cuts = [1024]
+                c0 = 0
+                for wd in cuts:
+                    units.append((h, c, c0, wd))
+                    c0 += wd
 
-        chunks = [(h, c) for h in range(HALVES) for c in range(PASSES)]
-        wr0 = load_w(*chunks[0])
-        pre = {0: split_w(wr0)}
+        pre = {}
+
+        def prepare(n):
+            h, c, c0, wd = units[n]
+            pre[n] = scalar_part(load_w(h, c, c0, wd), wd)
+
+        prepare(0)
+        prepare(1)
         for c in range(PASSES):
             g_pass(c)
 
         acc = {}
-        for n, (h, c) in enumerate(chunks):
-            if n + 1 < len(chunks):
-                pre[n + 1] = split_w(load_w(*chunks[n + 1]))
-            ag, sg = pre.pop(n)
-            a = ag[:].rearrange("p w t -> p (w t)")
-            f = [tmp.tile([P, 4 * W], BF16, name="f%d" % k) for k in range(5)]
-            plane(f[0][:], a, 0)
-            plane(f[1][:], a, 1)
-            plane(f[2][:], a, 2)
-            plane(f[3][:], a, 3)
-            vmax(f[0][:], f[0][:], f[1][:])
-            vmax(f[2][:], f[2][:], f[3][:])
-            plane(f[1][:], a, 4)
-            plane(f[3][:], a, 5)
-            plane(f[4][:], a, 6)
-            vmax(f[0][:], f[0][:], f[2][:])
-            vmax(f[1][:], f[1][:], f[3][:])
-            vmax(f[0][:], f[0][:], f[4][:])
-            vmax(f[0][:], f[0][:], f[1][:])
+        code_tiles = {}
+        evac = [0]
+        for n, (h, c, c0, wd) in enumerate(units):
+            if n + 2 < len(units):
+                prepare(n + 2)
+            ag, sg, y0, y1 = pre.pop(n)
+            m = 4 * wd
+            y2 = tmp.tile([P, 4 * W], BF16, name="y2")
+            f7 = tmp.tile([P, 4 * W], BF16, name="f7")
+            ts(y2[:, :m], ag[:, :m], col(2), col(5), ALU.mult, ALU.add)
+            ts(f7[:, :m], ag[:, :m], col(12), col(13), ALU.is_ge, ALU.mult)
+            ts(y0[:, :m], y0[:, :m], MAGIC, MAGIC, ALU.add, ALU.subtract)
+            ts(y2[:, :m], y2[:, :m], MAGIC, MAGIC, ALU.add, ALU.subtract)
+            ts(y1[:, :m], y1[:, :m], MAGIC, MAGIC, ALU.add, ALU.subtract)
+            ts(y0[:, :m], y0[:, :m], col(6), col(9), ALU.mult, ALU.min)
+            ts(y2[:, :m], y2[:, :m], col(8), col(11), ALU.mult, ALU.min)
+            ts(y1[:, :m], y1[:, :m], col(7), col(10), ALU.mult, ALU.min)
+            vmax(y2[:, :m], y2[:, :m], f7[:, :m])
+            vmax(y0[:, :m], y0[:, :m], y1[:, :m])
+            vmax(y0[:, :m], y0[:, :m], y2[:, :m])
             wq = two.tile([P, 4 * W], BF16, name="wq", align_bytes=64)
-            nc.vector.tensor_tensor(out=wq[:], in0=f[0][:], in1=sg[:].rearrange("p w t -> p (w t)"), op=ALU.mult)
-            w_codes = two.tile([P, W], U32, name="w_codes", align_bytes=64)
-            w_scales = two.tile([P, W], U8, name="w_scales", align_bytes=64)
-            nc.vector.quantize_mx(out=w_codes[:].bitcast(E4X4), scales=w_scales[:], in_=wq[:])
-            for it in range(I_TILES):
+            nc.vector.tensor_tensor(out=wq[:, :m], in0=y0[:, :m], in1=sg[:, :m], op=ALU.mult)
+            if c0 == 0:
+                w_codes = two.tile([P, W], U32, name="w_codes", align_bytes=64)
+                w_scales = two.tile([P, W], U8, name="w_scales", align_bytes=64)
+                code_tiles[0] = (w_codes, w_scales)
+            w_codes, w_scales = code_tiles[0]
+            nc.vector.quantize_mx(out=w_codes[:, c0:c0 + wd].bitcast(E4X4), scales=w_scales[:, c0:c0 + wd],
+                                  in_=wq[:, :m])
+            done = [it for it in range(I_TILES) if c0 < (it + 1) * N_TILE <= c0 + wd]
+            for it in done:
                 for s in range(S_TILES):
                     if c == 0:
                         acc[(s, it)] = psum.tile([P, 512], F32, name="bank")
@@ -149,10 +187,13 @@ def tile_primallinear_kernel(tc, x, weight, scale, grad_out, out):
                         start=(c == 0),
                         stop=(c == PASSES - 1),
                     )
-            if c == PASSES - 1:
-                for it in range(I_TILES):
+                if c == PASSES - 1:
                     for s in range(S_TILES):
                         res = ost.tile([P, N_TILE], F32, name="res")
-                        nc.scalar.copy(out=res[:], in_=acc[(s, it)][:])
-                        c0 = h * W + it * N_TILE
-                        nc.sync.dma_start(out=o2d[s * P:(s + 1) * P, c0:c0 + N_TILE], in_=res[:])
+                        if evac[0] % 2 == 0:
+                            nc.scalar.copy(out=res[:], in_=acc[(s, it)][:])
+                        else:
+                            nc.vector.tensor_copy(out=res[:], in_=acc[(s, it)][:])
+                        evac[0] += 1
+                        q0 = h * W + it * N_TILE
+                        nc.sync.dma_start(out=o2d[s * P:(s + 1) * P, q0:q0 + N_TILE], in_=res[:])

@@ -21,6 +21,7 @@ W = 1024
 HALVES = I // W
 N_TILE = 512
 I_TILES = W // N_TILE
+CHUNKS = HALVES * PASSES
 
 FLOPS = 2 * S * O * I
 BYTES = O * I * 2 + S * O * 2 + 2 + S * I * 4
@@ -29,6 +30,8 @@ VALUES = [0.076923, 0.090909, 0.142857, 0.2, 0.333333, 0.5, 1.0]
 EDGES = [0.0384521484375, 0.083740234375, 0.116943359375, 0.17138671875, 0.2666015625, 0.4169921875, 0.748046875]
 PAIRS = [(0, 1), (2, 3), (4, 5)]
 MAGIC = 12582912.0
+FIRST_CUTS = [128, 128, 256, 512]
+LAST_CUTS = [512, 512]
 
 
 def tile_primallinear_kernel(tc, x, weight, scale, grad_out, out):
@@ -41,6 +44,8 @@ def tile_primallinear_kernel(tc, x, weight, scale, grad_out, out):
         act_pool = ctx.enter_context(tc.tile_pool(name="actp", bufs=2))
         tmp = ctx.enter_context(tc.tile_pool(name="tmp", bufs=1))
         two = ctx.enter_context(tc.tile_pool(name="two", bufs=2))
+        gr_pool = ctx.enter_context(tc.tile_pool(name="gr", bufs=4))
+        gg_pool = ctx.enter_context(tc.tile_pool(name="gg", bufs=8))
         ost = ctx.enter_context(tc.tile_pool(name="ost", bufs=4))
         psum = ctx.enter_context(tc.psum_pool(name="ps", bufs=8))
 
@@ -70,47 +75,57 @@ def tile_primallinear_kernel(tc, x, weight, scale, grad_out, out):
         g_codes = keep.tile([P, PASSES, S], U32, align_bytes=64)
         g_scales = keep.tile([P, PASSES, S], U8, align_bytes=64)
 
-        def load_w(h, c, c0, wd):
-            wr = wr_pool.tile([P, 4, W], BF16, name="wr")
-            for u in range(2):
-                r0 = K_PASS * c + 256 * u
-                nc.sync.dma_start(
-                    out=wr[:, 2 * u:2 * u + 2, :wd],
-                    in_=weight[r0:r0 + 256, h * W + c0:h * W + c0 + wd].rearrange("(p e) w -> p e w", e=2),
-                )
-            return wr
+        def cuts_of(j):
+            if j == 0:
+                return FIRST_CUTS
+            if j == CHUNKS - 1:
+                return LAST_CUTS
+            return [W]
 
-        def scalar_part(wr, wd):
-            n = 4 * wd
+        units = []
+        for j in range(CHUNKS):
+            c0 = 0
+            for wd in cuts_of(j):
+                units.append((j, c0, wd, 0 if j == 0 else 2))
+                c0 += wd
+        first = len(FIRST_CUTS)
+
+        raw = {}
+
+        def load(j):
+            if j >= CHUNKS:
+                return
+            h, c = divmod(j, PASSES)
+            wr = wr_pool.tile([P, 4, W], BF16, name="wr")
+            raw[j] = wr
+            c0 = 0
+            for wd in cuts_of(j):
+                for u in range(2):
+                    r0 = K_PASS * c + 256 * u
+                    nc.sync.dma_start(
+                        out=wr[:, 2 * u:2 * u + 2, c0:c0 + wd],
+                        in_=weight[r0:r0 + 256, h * W + c0:h * W + c0 + wd].rearrange("(p e) w -> p e w", e=2),
+                    )
+                c0 += wd
+
+        pre = {}
+
+        def act(n):
+            if n >= len(units):
+                return
+            j, c0, wd, ka = units[n]
+            m = 4 * wd
             ag = act_pool.tile([P, 4 * W], BF16, name="ag")
             sg = act_pool.tile([P, 4 * W], BF16, name="sg")
             y0 = act_pool.tile([P, 4 * W], BF16, name="y0")
             y1 = act_pool.tile([P, 4 * W], BF16, name="y1")
-            src = wr[:, :, :wd].rearrange("p t (c i) -> p c t i", i=4)
-            nc.scalar.activation(out=ag[:, :n].rearrange("p (c i t) -> p c t i", i=4, t=4), in_=src, func=ACT.Abs)
-            nc.scalar.activation(out=y0[:, :n], in_=ag[:, :n], func=ACT.Identity, scale=col(0), bias=col(3))
-            nc.scalar.activation(out=y1[:, :n], in_=ag[:, :n], func=ACT.Identity, scale=col(1), bias=col(4))
-            nc.scalar.activation(out=sg[:, :n].rearrange("p (c i t) -> p c t i", i=4, t=4), in_=src, func=ACT.Sign)
-            return ag, sg, y0, y1
-
-        def g_pass(c):
-            gr = wr_pool.tile([P, 4, W], BF16, name="wr")
-            nc.sync.dma_start(out=gr[:, :, :K_PASS],
-                              in_=g2d[:, K_PASS * c:K_PASS * (c + 1)].rearrange("(s p) k -> p s k", p=P))
-            gg = two.tile([P, 4 * W], BF16, name="wq", align_bytes=64)
-            ggw = gg[:, :4 * S].bitcast(F32)
-            for sp in range(2):
-                tp = psum.tile([P, 512], F32, name="bank")
-                for s2 in range(2):
-                    words = gr[:, 2 * sp + s2, :K_PASS].bitcast(F32)
-                    for u in range(2):
-                        o0 = (2 * s2 + u) * P
-                        nc.tensor.transpose(tp[:, o0:o0 + P], words[:, P * u:P * (u + 1)], ident[:])
-                nc.vector.tensor_copy(
-                    out=ggw[:, sp * 512:(sp + 1) * 512].rearrange("p (s r u) -> p s r u", s=2, u=2),
-                    in_=tp[:].rearrange("p (s u r) -> p s r u", s=2, u=2),
-                )
-            nc.vector.quantize_mx(out=g_codes[:, c, :].bitcast(E5X4), scales=g_scales[:, c, :], in_=gg[:, :4 * S])
+            ys = [y0, y1]
+            src = raw[j][:, :, c0:c0 + wd].rearrange("p t (c i) -> p c t i", i=4)
+            nc.scalar.activation(out=ag[:, :m].rearrange("p (c i t) -> p c t i", i=4, t=4), in_=src, func=ACT.Abs)
+            for k in range(ka):
+                nc.scalar.activation(out=ys[k][:, :m], in_=ag[:, :m], func=ACT.Identity, scale=col(k), bias=col(3 + k))
+            nc.scalar.activation(out=sg[:, :m].rearrange("p (c i t) -> p c t i", i=4, t=4), in_=src, func=ACT.Sign)
+            pre[n] = (ag, sg, y0, y1)
 
         def ts(dst, src, s1, s2, op0, op1):
             nc.vector.tensor_scalar(out=dst, in0=src, scalar1=s1, scalar2=s2, op0=op0, op1=op1)
@@ -118,82 +133,112 @@ def tile_primallinear_kernel(tc, x, weight, scale, grad_out, out):
         def vmax(dst, a, b):
             nc.vector.tensor_tensor(out=dst, in0=a, in1=b, op=ALU.max)
 
-        units = []
-        for h in range(HALVES):
-            for c in range(PASSES):
-                if (h, c) == (0, 0):
-                    cuts = [256, 256, 512]
-                elif (h, c) == (HALVES - 1, PASSES - 1):
-                    cuts = [512, 512]
-                else:
-                    cuts = [1024]
-                c0 = 0
-                for wd in cuts:
-                    units.append((h, c, c0, wd))
-                    c0 += wd
+        codes = {}
 
-        pre = {}
-
-        def prepare(n):
-            h, c, c0, wd = units[n]
-            pre[n] = scalar_part(load_w(h, c, c0, wd), wd)
-
-        prepare(0)
-        prepare(1)
-        for c in range(PASSES):
-            g_pass(c)
-
-        acc = {}
-        code_tiles = {}
-        evac = [0]
-        for n, (h, c, c0, wd) in enumerate(units):
-            if n + 2 < len(units):
-                prepare(n + 2)
+        def dve(n):
+            j, c0, wd, ka = units[n]
             ag, sg, y0, y1 = pre.pop(n)
             m = 4 * wd
             y2 = tmp.tile([P, 4 * W], BF16, name="y2")
             f7 = tmp.tile([P, 4 * W], BF16, name="f7")
-            ts(y2[:, :m], ag[:, :m], col(2), col(5), ALU.mult, ALU.add)
+            m01 = tmp.tile([P, 4 * W], BF16, name="m01")
+            ys = [y0, y1, y2]
+            for k in range(2, ka - 1, -1):
+                ts(ys[k][:, :m], ag[:, :m], col(k), col(3 + k), ALU.mult, ALU.add)
             ts(f7[:, :m], ag[:, :m], col(12), col(13), ALU.is_ge, ALU.mult)
-            ts(y0[:, :m], y0[:, :m], MAGIC, MAGIC, ALU.add, ALU.subtract)
-            ts(y2[:, :m], y2[:, :m], MAGIC, MAGIC, ALU.add, ALU.subtract)
-            ts(y1[:, :m], y1[:, :m], MAGIC, MAGIC, ALU.add, ALU.subtract)
-            ts(y0[:, :m], y0[:, :m], col(6), col(9), ALU.mult, ALU.min)
-            ts(y2[:, :m], y2[:, :m], col(8), col(11), ALU.mult, ALU.min)
-            ts(y1[:, :m], y1[:, :m], col(7), col(10), ALU.mult, ALU.min)
+            for k in range(3):
+                ts(ys[k][:, :m], ys[k][:, :m], MAGIC, MAGIC, ALU.add, ALU.subtract)
+            for k in range(3):
+                ts(ys[k][:, :m], ys[k][:, :m], col(6 + k), col(9 + k), ALU.mult, ALU.min)
+            vmax(m01[:, :m], y0[:, :m], y1[:, :m])
             vmax(y2[:, :m], y2[:, :m], f7[:, :m])
-            vmax(y0[:, :m], y0[:, :m], y1[:, :m])
-            vmax(y0[:, :m], y0[:, :m], y2[:, :m])
+            vmax(m01[:, :m], m01[:, :m], y2[:, :m])
             wq = two.tile([P, 4 * W], BF16, name="wq", align_bytes=64)
-            nc.vector.tensor_tensor(out=wq[:, :m], in0=y0[:, :m], in1=sg[:, :m], op=ALU.mult)
+            nc.vector.tensor_tensor(out=wq[:, :m], in0=m01[:, :m], in1=sg[:, :m], op=ALU.mult)
             if c0 == 0:
                 w_codes = two.tile([P, W], U32, name="w_codes", align_bytes=64)
                 w_scales = two.tile([P, W], U8, name="w_scales", align_bytes=64)
-                code_tiles[0] = (w_codes, w_scales)
-            w_codes, w_scales = code_tiles[0]
+                codes[j] = (w_codes, w_scales)
+            w_codes, w_scales = codes[j]
             nc.vector.quantize_mx(out=w_codes[:, c0:c0 + wd].bitcast(E4X4), scales=w_scales[:, c0:c0 + wd],
                                   in_=wq[:, :m])
-            done = [it for it in range(I_TILES) if c0 < (it + 1) * N_TILE <= c0 + wd]
-            for it in done:
-                for s in range(S_TILES):
-                    if c == 0:
-                        acc[(s, it)] = psum.tile([P, 512], F32, name="bank")
-                    nc.tensor.matmul_mx(
-                        out=acc[(s, it)][:],
-                        lhsT=g_codes[:, c, s * P:(s + 1) * P].bitcast(E5X4),
-                        lhsT_scale=g_scales[:, c, s * P:(s + 1) * P],
-                        rhs=w_codes[:, it * N_TILE:(it + 1) * N_TILE].bitcast(E4X4),
-                        rhs_scale=w_scales[:, it * N_TILE:(it + 1) * N_TILE],
-                        start=(c == 0),
-                        stop=(c == PASSES - 1),
-                    )
-                if c == PASSES - 1:
-                    for s in range(S_TILES):
-                        res = ost.tile([P, N_TILE], F32, name="res")
-                        if evac[0] % 2 == 0:
-                            nc.scalar.copy(out=res[:], in_=acc[(s, it)][:])
-                        else:
-                            nc.vector.tensor_copy(out=res[:], in_=acc[(s, it)][:])
-                        evac[0] += 1
-                        q0 = h * W + it * N_TILE
-                        nc.sync.dma_start(out=o2d[s * P:(s + 1) * P, q0:q0 + N_TILE], in_=res[:])
+
+        acc = {}
+
+        def mx(j, it):
+            h, c = divmod(j, PASSES)
+            w_codes, w_scales = codes[j]
+            for s in range(S_TILES):
+                if c == 0:
+                    acc[(s, it)] = psum.tile([P, 512], F32, name="bank")
+                nc.tensor.matmul_mx(
+                    out=acc[(s, it)][:],
+                    lhsT=g_codes[:, c, s * P:(s + 1) * P].bitcast(E5X4),
+                    lhsT_scale=g_scales[:, c, s * P:(s + 1) * P],
+                    rhs=w_codes[:, it * N_TILE:(it + 1) * N_TILE].bitcast(E4X4),
+                    rhs_scale=w_scales[:, it * N_TILE:(it + 1) * N_TILE],
+                    start=(c == 0),
+                    stop=(c == PASSES - 1),
+                )
+
+        def empty(j, it, share):
+            h, c = divmod(j, PASSES)
+            for s in range(S_TILES):
+                res = ost.tile([P, N_TILE], F32, name="res")
+                q0 = h * W + it * N_TILE
+                if share and s % 2 == 1:
+                    nc.vector.tensor_copy(out=res[:], in_=acc[(s, it)][:])
+                    nc.sync.dma_start(out=o2d[s * P:(s + 1) * P, q0:q0 + N_TILE], in_=res[:])
+                else:
+                    nc.scalar.copy(out=res[:], in_=acc[(s, it)][:])
+                    nc.scalar.dma_start(out=o2d[s * P:(s + 1) * P, q0:q0 + N_TILE], in_=res[:])
+
+        load(0)
+        g_raw = []
+        for c in range(PASSES):
+            gr = gr_pool.tile([P, S_TILES, K_PASS], BF16, name="gr")
+            nc.sync.dma_start(out=gr[:], in_=g2d[:, K_PASS * c:K_PASS * (c + 1)].rearrange("(s p) k -> p s k", p=P))
+            g_raw.append(gr)
+        load(1)
+        load(2)
+        act(0)
+        act(1)
+        for n in range(first):
+            if n + 2 < first:
+                act(n + 2)
+            dve(n)
+        g_grouped = []
+        for c in range(PASSES):
+            gg = gg_pool.tile([P, 4 * S], BF16, name="gg", align_bytes=64)
+            g_grouped.append(gg)
+            ggw = gg[:].bitcast(F32)
+            for sp in range(2):
+                tp = psum.tile([P, 512], F32, name="bank")
+                for s2 in range(2):
+                    words = g_raw[c][:, 2 * sp + s2, :].bitcast(F32)
+                    for u in range(2):
+                        o0 = (2 * s2 + u) * P
+                        nc.tensor.transpose(tp[:, o0:o0 + P], words[:, P * u:P * (u + 1)], ident[:])
+                nc.scalar.copy(
+                    out=ggw[:, sp * 512:(sp + 1) * 512].rearrange("p (s r u) -> p s r u", s=2, u=2),
+                    in_=tp[:].rearrange("p (s u r) -> p s r u", s=2, u=2),
+                )
+        act(first)
+        act(first + 1)
+        for c in range(PASSES):
+            nc.vector.quantize_mx(out=g_codes[:, c, :].bitcast(E5X4), scales=g_scales[:, c, :], in_=g_grouped[c][:])
+        mx(0, 0)
+        mx(0, 1)
+
+        for n in range(first, len(units)):
+            j, c0, wd, ka = units[n]
+            if c0 == 0:
+                load(j + 2)
+            act(n + 2)
+            dve(n)
+            last = j == CHUNKS - 1
+            for it in range(I_TILES):
+                if c0 < (it + 1) * N_TILE <= c0 + wd:
+                    mx(j, it)
+                    if j % PASSES == PASSES - 1:
+                        empty(j, it, last and it == I_TILES - 1)

@@ -146,13 +146,21 @@ def tile_primallinear_kernel(tc, x, weight, scale, grad_out, out):
             for k in range(2, ka - 1, -1):
                 ts(ys[k][:, :m], ag[:, :m], col(k), col(3 + k), ALU.mult, ALU.add)
             ts(f7[:, :m], ag[:, :m], col(12), col(13), ALU.is_ge, ALU.mult)
-            for k in range(3):
+            def rnd(k):
                 ts(ys[k][:, :m], ys[k][:, :m], MAGIC, MAGIC, ALU.add, ALU.subtract)
-            for k in range(3):
+
+            def val(k):
                 ts(ys[k][:, :m], ys[k][:, :m], col(6 + k), col(9 + k), ALU.mult, ALU.min)
-            vmax(m01[:, :m], y0[:, :m], y1[:, :m])
+
+            rnd(2)
+            rnd(0)
+            val(2)
+            val(0)
             vmax(y2[:, :m], y2[:, :m], f7[:, :m])
-            vmax(m01[:, :m], m01[:, :m], y2[:, :m])
+            rnd(1)
+            vmax(m01[:, :m], y0[:, :m], y2[:, :m])
+            val(1)
+            vmax(m01[:, :m], m01[:, :m], y1[:, :m])
             wq = two.tile([P, 4 * W], BF16, name="wq", align_bytes=64)
             nc.vector.tensor_tensor(out=wq[:, :m], in0=m01[:, :m], in1=sg[:, :m], op=ALU.mult)
             if c0 == 0:

from contextlib import ExitStack

import concourse.mybir as mybir
from concourse.masks import make_identity

F32 = mybir.dt.float32
BF16 = mybir.dt.bfloat16
U32 = mybir.dt.uint32
U8 = mybir.dt.uint8
E4X4 = mybir.dt.float8_e4m3fn_x4
E5X4 = mybir.dt.float8_e5m2_x4
ALU = mybir.AluOpType
ACT = mybir.ActivationFunctionType

P = 128
S, O, I = 512, 4096, 2048
K_PASS = 512
PASSES = O // K_PASS
S_TILES = S // P
W = 1024
HALVES = I // W
N_TILE = 512
I_TILES = W // N_TILE
CHUNKS = HALVES * PASSES

FLOPS = 2 * S * O * I
BYTES = O * I * 2 + S * O * 2 + 2 + S * I * 4

VALUES = [0.076923, 0.090909, 0.142857, 0.2, 0.333333, 0.5, 1.0]
EDGES = [0.0384521484375, 0.083740234375, 0.116943359375, 0.17138671875, 0.2666015625, 0.4169921875, 0.748046875]
PAIRS = [(0, 1), (2, 3), (4, 5)]
MAGIC = 12582912.0
FIRST_CUTS = [128, 128, 256, 512]
LAST_CUTS = [512, 512]


def tile_primallinear_kernel(tc, x, weight, scale, grad_out, out):
    nc = tc.nc
    g2d = grad_out.rearrange("b s o -> (b s) o")
    o2d = out.rearrange("b s i -> (b s) i")
    with ExitStack() as ctx:
        keep = ctx.enter_context(tc.tile_pool(name="keep", bufs=1))
        wr_pool = ctx.enter_context(tc.tile_pool(name="wr", bufs=3))
        act_pool = ctx.enter_context(tc.tile_pool(name="actp", bufs=2))
        tmp = ctx.enter_context(tc.tile_pool(name="tmp", bufs=1))
        two = ctx.enter_context(tc.tile_pool(name="two", bufs=2))
        gr_pool = ctx.enter_context(tc.tile_pool(name="gr", bufs=4))
        gg_pool = ctx.enter_context(tc.tile_pool(name="gg", bufs=8))
        ost = ctx.enter_context(tc.tile_pool(name="ost", bufs=4))
        psum = ctx.enter_context(tc.psum_pool(name="ps", bufs=8))

        sc_bf = keep.tile([P, 1], BF16)
        nc.sync.dma_start(out=sc_bf[:], in_=scale.partition_broadcast(P))
        sc = keep.tile([P, 1], F32)
        nc.vector.tensor_copy(out=sc[:], in_=sc_bf[:])
        inv = keep.tile([P, 1], F32)
        nc.vector.reciprocal(out=inv[:], in_=sc[:])
        cst = keep.tile([P, 16], F32)

        def col(j):
            return cst[:, j:j + 1]

        for k, (lo, hi) in enumerate(PAIRS):
            h = EDGES[hi] - EDGES[lo]
            nc.vector.tensor_scalar(out=col(k), in0=inv[:, 0:1], scalar1=1.0 / h, scalar2=None, op0=ALU.mult)
            nc.vector.tensor_scalar(out=col(3 + k), in0=sc[:, 0:1], scalar1=0.0, scalar2=0.5 - EDGES[lo] / h,
                                    op0=ALU.mult, op1=ALU.add)
            nc.vector.tensor_scalar(out=col(6 + k), in0=sc[:, 0:1], scalar1=VALUES[lo], scalar2=None, op0=ALU.mult)
            nc.vector.tensor_scalar(out=col(9 + k), in0=sc[:, 0:1], scalar1=VALUES[hi], scalar2=None, op0=ALU.mult)
        nc.vector.tensor_scalar(out=col(12), in0=sc[:, 0:1], scalar1=EDGES[6], scalar2=None, op0=ALU.mult)
        nc.vector.tensor_scalar(out=col(13), in0=sc[:, 0:1], scalar1=VALUES[6], scalar2=None, op0=ALU.mult)
        ident = keep.tile([P, P], F32)
        make_identity(nc, ident[:])

        g_codes = keep.tile([P, PASSES, S], U32, align_bytes=64)
        g_scales = keep.tile([P, PASSES, S], U8, align_bytes=64)

        def cuts_of(j):
            if j == 0:
                return FIRST_CUTS
            if j == CHUNKS - 1:
                return LAST_CUTS
            return [W]

        units = []
        for j in range(CHUNKS):
            c0 = 0
            for wd in cuts_of(j):
                units.append((j, c0, wd, 0 if j == 0 else 2))
                c0 += wd
        first = len(FIRST_CUTS)

        raw = {}

        def load(j):
            if j >= CHUNKS:
                return
            h, c = divmod(j, PASSES)
            wr = wr_pool.tile([P, 4, W], BF16, name="wr")
            raw[j] = wr
            c0 = 0
            for wd in cuts_of(j):
                for u in range(2):
                    r0 = K_PASS * c + 256 * u
                    nc.sync.dma_start(
                        out=wr[:, 2 * u:2 * u + 2, c0:c0 + wd],
                        in_=weight[r0:r0 + 256, h * W + c0:h * W + c0 + wd].rearrange("(p e) w -> p e w", e=2),
                    )
                c0 += wd

        pre = {}

        def act(n):
            if n >= len(units):
                return
            j, c0, wd, ka = units[n]
            m = 4 * wd
            ag = act_pool.tile([P, 4 * W], BF16, name="ag")
            sg = act_pool.tile([P, 4 * W], BF16, name="sg")
            y0 = act_pool.tile([P, 4 * W], BF16, name="y0")
            y1 = act_pool.tile([P, 4 * W], BF16, name="y1")
            ys = [y0, y1]
            src = raw[j][:, :, c0:c0 + wd].rearrange("p t (c i) -> p c t i", i=4)
            nc.scalar.activation(out=ag[:, :m].rearrange("p (c i t) -> p c t i", i=4, t=4), in_=src, func=ACT.Abs)
            for k in range(ka):
                nc.scalar.activation(out=ys[k][:, :m], in_=ag[:, :m], func=ACT.Identity, scale=col(k), bias=col(3 + k))
            nc.scalar.activation(out=sg[:, :m].rearrange("p (c i t) -> p c t i", i=4, t=4), in_=src, func=ACT.Sign)
            pre[n] = (ag, sg, y0, y1)

        def ts(dst, src, s1, s2, op0, op1):
            nc.vector.tensor_scalar(out=dst, in0=src, scalar1=s1, scalar2=s2, op0=op0, op1=op1)

        def vmax(dst, a, b):
            nc.vector.tensor_tensor(out=dst, in0=a, in1=b, op=ALU.max)

        codes = {}

        def dve(n):
            j, c0, wd, ka = units[n]
            ag, sg, y0, y1 = pre.pop(n)
            m = 4 * wd
            y2 = tmp.tile([P, 4 * W], BF16, name="y2")
            f7 = tmp.tile([P, 4 * W], BF16, name="f7")
            m01 = tmp.tile([P, 4 * W], BF16, name="m01")
            ys = [y0, y1, y2]
            for k in range(2, ka - 1, -1):
                ts(ys[k][:, :m], ag[:, :m], col(k), col(3 + k), ALU.mult, ALU.add)
            ts(f7[:, :m], ag[:, :m], col(12), col(13), ALU.is_ge, ALU.mult)
            def rnd(k):
                ts(ys[k][:, :m], ys[k][:, :m], MAGIC, MAGIC, ALU.add, ALU.subtract)

            def val(k):
                ts(ys[k][:, :m], ys[k][:, :m], col(6 + k), col(9 + k), ALU.mult, ALU.min)

            rnd(2)
            rnd(0)
            val(2)
            val(0)
            vmax(y2[:, :m], y2[:, :m], f7[:, :m])
            rnd(1)
            vmax(m01[:, :m], y0[:, :m], y2[:, :m])
            val(1)
            vmax(m01[:, :m], m01[:, :m], y1[:, :m])
            wq = two.tile([P, 4 * W], BF16, name="wq", align_bytes=64)
            nc.vector.tensor_tensor(out=wq[:, :m], in0=m01[:, :m], in1=sg[:, :m], op=ALU.mult)
            if c0 == 0:
                w_codes = two.tile([P, W], U32, name="w_codes", align_bytes=64)
                w_scales = two.tile([P, W], U8, name="w_scales", align_bytes=64)
                codes[j] = (w_codes, w_scales)
            w_codes, w_scales = codes[j]
            nc.vector.quantize_mx(out=w_codes[:, c0:c0 + wd].bitcast(E4X4), scales=w_scales[:, c0:c0 + wd],
                                  in_=wq[:, :m])

        acc = {}

        def mx(j, it):
            h, c = divmod(j, PASSES)
            w_codes, w_scales = codes[j]
            for s in range(S_TILES):
                if c == 0:
                    acc[(s, it)] = psum.tile([P, 512], F32, name="bank")
                nc.tensor.matmul_mx(
                    out=acc[(s, it)][:],
                    lhsT=g_codes[:, c, s * P:(s + 1) * P].bitcast(E5X4),
                    lhsT_scale=g_scales[:, c, s * P:(s + 1) * P],
                    rhs=w_codes[:, it * N_TILE:(it + 1) * N_TILE].bitcast(E4X4),
                    rhs_scale=w_scales[:, it * N_TILE:(it + 1) * N_TILE],
                    start=(c == 0),
                    stop=(c == PASSES - 1),
                )

        def empty(j, it, share):
            h, c = divmod(j, PASSES)
            for s in range(S_TILES):
                res = ost.tile([P, N_TILE], F32, name="res")
                q0 = h * W + it * N_TILE
                if share and s % 2 == 1:
                    nc.vector.tensor_copy(out=res[:], in_=acc[(s, it)][:])
                    nc.sync.dma_start(out=o2d[s * P:(s + 1) * P, q0:q0 + N_TILE], in_=res[:])
                else:
                    nc.scalar.copy(out=res[:], in_=acc[(s, it)][:])
                    nc.scalar.dma_start(out=o2d[s * P:(s + 1) * P, q0:q0 + N_TILE], in_=res[:])

        load(0)
        g_raw = []
        for c in range(PASSES):
            gr = gr_pool.tile([P, S_TILES, K_PASS], BF16, name="gr")
            nc.sync.dma_start(out=gr[:], in_=g2d[:, K_PASS * c:K_PASS * (c + 1)].rearrange("(s p) k -> p s k", p=P))
            g_raw.append(gr)
        load(1)
        load(2)
        act(0)
        act(1)
        for n in range(first):
            if n + 2 < first:
                act(n + 2)
            dve(n)
        g_grouped = []
        for c in range(PASSES):
            gg = gg_pool.tile([P, 4 * S], BF16, name="gg", align_bytes=64)
            g_grouped.append(gg)
            ggw = gg[:].bitcast(F32)
            for sp in range(2):
                tp = psum.tile([P, 512], F32, name="bank")
                for s2 in range(2):
                    words = g_raw[c][:, 2 * sp + s2, :].bitcast(F32)
                    for u in range(2):
                        o0 = (2 * s2 + u) * P
                        nc.tensor.transpose(tp[:, o0:o0 + P], words[:, P * u:P * (u + 1)], ident[:])
                nc.scalar.copy(
                    out=ggw[:, sp * 512:(sp + 1) * 512].rearrange("p (s r u) -> p s r u", s=2, u=2),
                    in_=tp[:].rearrange("p (s u r) -> p s r u", s=2, u=2),
                )
        act(first)
        act(first + 1)
        for c in range(PASSES):
            nc.vector.quantize_mx(out=g_codes[:, c, :].bitcast(E5X4), scales=g_scales[:, c, :], in_=g_grouped[c][:])
        mx(0, 0)
        mx(0, 1)

        for n in range(first, len(units)):
            j, c0, wd, ka = units[n]
            if c0 == 0:
                load(j + 2)
            act(n + 2)
            dve(n)
            last = j == CHUNKS - 1
            for it in range(I_TILES):
                if c0 < (it + 1) * N_TILE <= c0 + wd:
                    mx(j, it)
                    if j % PASSES == PASSES - 1:
                        empty(j, it, last and it == I_TILES - 1)
